import numpy as np
import ml_dtypes


def mxq(x, axis, fmt="e4m3"):
    dtype, down = {"e4m3": (ml_dtypes.float8_e4m3fn, 7), "e5m2": (ml_dtypes.float8_e5m2, 14)}[fmt]
    v = np.moveaxis(np.asarray(x, np.float32).astype(ml_dtypes.bfloat16).astype(np.float64), axis, -1)
    blocks = v.reshape(v.shape[:-1] + (-1, 32))
    amax = np.abs(blocks).max(-1, keepdims=True)
    byte = np.maximum(np.where(amax > 0, np.frexp(amax)[1] - 1 + 127, 0) - down, 1)
    scale = np.exp2(byte - 127.0)
    codes = (blocks / scale).astype(np.float32).astype(dtype).astype(np.float64)
    return np.moveaxis((codes * scale).reshape(v.shape), -1, axis)


WIDE = False


def mx_kscale(k):
    if not WIDE:
        return np.ones(k)
    levels = np.array([20, -20, 10, -10, 0])
    a = np.random.permutation(np.resize(levels, k // 512 * 4)).reshape(k // 512, 4)
    idx = np.arange(k)
    return np.exp2(a[idx // 512, idx % 128 // 32])


BF16 = ml_dtypes.bfloat16


def bf(x):
    return np.asarray(x, np.float32).astype(BF16)


def f64(x):
    return np.asarray(x).astype(np.float64)


N, LMAX, CIN, COUT = 512, 3, 256, 1024
NL = LMAX + 1
NM = NL * NL


def setup_inputs():
    u = mx_kscale(COUT)
    x = np.random.standard_normal((N, NM, CIN))
    weights = np.random.standard_normal((NL, CIN, COUT)) / np.sqrt(CIN) / u
    path_weights = 1.0 + 0.3 * np.random.standard_normal(NL)
    g = np.random.standard_normal((N, NM, COUT)) * np.exp2(np.random.randint(-12, 1, (N, NM, 1))) * 16.0 * u
    return {"x": bf(x), "weights": bf(weights), "path_weights": bf(path_weights), "grad_out": bf(g)}


def reference(x, weights, path_weights, grad_out):
    weights, path_weights, g = f64(weights), f64(path_weights), f64(grad_out)
    blocks = []
    for l in range(LMAX + 1):
        start = l * l
        end = start + (2 * l + 1)
        blk = mxq(g[:, start:end, :], 2, "e5m2") @ mxq(weights[l], 1, "e4m3").T
        blocks.append(path_weights[l] * blk)
    return np.concatenate(blocks, axis=1)

@@ -1,0 +1,155 @@
+from contextlib import ExitStack
+
+import concourse.mybir as mybir
+from concourse.masks import make_identity
+
+F32 = mybir.dt.float32
+BF16 = mybir.dt.bfloat16
+U32 = mybir.dt.uint32
+U8 = mybir.dt.uint8
+E4M3_X4 = mybir.dt.float8_e4m3fn_x4
+E5M2_X4 = mybir.dt.float8_e5m2_x4
+
+P = 128
+NODES, DEGREES, CIN, K = 512, 4, 256, 1024
+ROWS = DEGREES * DEGREES
+DEGREE_OF_ROW = [l for l in range(DEGREES) for row in range(2 * l + 1)]
+
+K_PASS = 4 * P
+PASSES = K // K_PASS
+QUARTERS = K // 2 // P
+TILES = 4
+CHUNK_WORDS = TILES * PASSES * P
+W_CHUNKS = DEGREES * CIN // (TILES * P)
+DEGREES_PER_W_CHUNK = DEGREES // W_CHUNKS
+NODE_GROUPS = NODES // P
+ROW_GROUPS = ROWS // TILES
+G_CHUNKS = NODE_GROUPS * ROW_GROUPS
+N_MOVING = DEGREES_PER_W_CHUNK * CIN
+
+FLOPS = 2 * NODES * ROWS * CIN * K
+BYTES = 2 * NODES * ROWS * K + 2 * DEGREES * CIN * K + 2 * DEGREES + 4 * NODES * ROWS * CIN
+
+
+def tile_linear_pa_kernel(tc, x, weights, path_weights, grad_out, out):
+    nc = tc.nc
+    assert tuple(grad_out.shape) == (NODES, ROWS, K)
+    assert tuple(weights.shape) == (DEGREES, CIN, K)
+    assert tuple(out.shape) == (NODES, ROWS, CIN)
+
+    with ExitStack() as ctx:
+        ctx.enter_context(tc.manual_schedule())
+        const = ctx.enter_context(tc.tile_pool(name="const", bufs=1))
+        raw_pool = ctx.enter_context(tc.tile_pool(name="raw", bufs=W_CHUNKS + G_CHUNKS))
+        grouped_pool = ctx.enter_context(tc.tile_pool(name="grouped", bufs=2))
+        codes_pool = ctx.enter_context(tc.tile_pool(name="codes", bufs=2))
+        result_pool = ctx.enter_context(tc.tile_pool(name="result", bufs=6))
+        words_psum = ctx.enter_context(tc.psum_pool(name="words_psum", bufs=TILES))
+        acc_psum = ctx.enter_context(tc.psum_pool(name="acc_psum", bufs=TILES))
+
+        def load_weights(chunk):
+            raw = raw_pool.tile([P, TILES * K], BF16, name="raw")
+            w_rows = weights.rearrange("l c k -> (l c) k")[chunk * TILES * P : (chunk + 1) * TILES * P, :]
+            nc.sync.dma_start(
+                out=raw[:].rearrange("p (t k) -> p t k", t=TILES),
+                in_=w_rows.rearrange("(t p) k -> p t k", p=P),
+            )
+            return raw
+
+        def load_grad(chunk):
+            node_group, row_group = divmod(chunk, ROW_GROUPS)
+            raw = raw_pool.tile([P, TILES * K], BF16, name="raw")
+            nc.sync.dma_start(
+                out=raw[:],
+                in_=grad_out.rearrange("n m k -> n (m k)")[
+                    node_group * P : (node_group + 1) * P,
+                    row_group * TILES * K : (row_group + 1) * TILES * K,
+                ],
+            )
+            return raw
+
+        w_raw = [load_weights(0)]
+        g_raw = [load_grad(0)]
+        w_raw.extend(load_weights(chunk) for chunk in range(1, W_CHUNKS))
+        g_raw.extend(load_grad(chunk) for chunk in range(1, G_CHUNKS))
+
+        identity = const.tile([P, P], F32)
+        make_identity(nc, identity[:])
+        factor_bf16 = const.tile([P, DEGREES], BF16)
+        nc.scalar.dma_start(out=factor_bf16[:], in_=path_weights.partition_broadcast(P))
+        factor = const.tile([P, DEGREES], F32)
+        nc.vector.tensor_copy(out=factor[:], in_=factor_bf16[:])
+
+        w_codes = const.tile([P, W_CHUNKS * CHUNK_WORDS], U32, align_bytes=64)
+        w_scales = const.tile([P, W_CHUNKS * CHUNK_WORDS], U8, align_bytes=64)
+
+        def quantise_chunk(raw, codes, scales, x4):
+            raw_words = raw[:].bitcast(F32)
+            grouped = grouped_pool.tile([P, 4 * CHUNK_WORDS], BF16, align_bytes=64)
+            grouped_words = grouped[:].bitcast(F32).rearrange(
+                "q (c t r u) -> q c t r u", c=PASSES, t=TILES, u=2
+            )
+            for t in range(TILES):
+                bank = words_psum.tile([P, QUARTERS, P], F32)
+                for h in range(QUARTERS):
+                    first = (t * QUARTERS + h) * P
+                    nc.tensor.transpose(bank[:, h, :], raw_words[:, first : first + P], identity[:])
+                nc.scalar.copy(
+                    out=grouped_words[:, :, t, :, :],
+                    in_=bank[:].rearrange("q (c u) r -> q c r u", u=2),
+                )
+            nc.vector.quantize_mx(out=codes.bitcast(x4), scales=scales, in_=grouped[:])
+
+        def quantise_weights(chunk):
+            columns = slice(chunk * CHUNK_WORDS, (chunk + 1) * CHUNK_WORDS)
+            quantise_chunk(w_raw[chunk], w_codes[:, columns], w_scales[:, columns], E4M3_X4)
+
+        def quantise_grad(chunk):
+            g_codes = codes_pool.tile([P, CHUNK_WORDS], U32, align_bytes=64)
+            g_scales = codes_pool.tile([P, CHUNK_WORDS], U8, align_bytes=64)
+            quantise_chunk(g_raw[chunk], g_codes[:], g_scales[:], E5M2_X4)
+            return g_codes, g_scales
+
+        def multiply(chunk, g_codes, g_scales):
+            node_group, row_group = divmod(chunk, ROW_GROUPS)
+            result = result_pool.tile([P, TILES, CIN], F32)
+            for t in range(TILES):
+                degree = DEGREE_OF_ROW[row_group * TILES + t]
+                w_chunk, place = divmod(degree, DEGREES_PER_W_CHUNK)
+                acc = acc_psum.tile([P, N_MOVING], F32)
+                for c in range(PASSES):
+                    g_columns = slice((c * TILES + t) * P, (c * TILES + t + 1) * P)
+                    w_first = w_chunk * CHUNK_WORDS + c * N_MOVING
+                    w_columns = slice(w_first, w_first + N_MOVING)
+                    nc.tensor.matmul_mx(
+                        out=acc[:],
+                        lhsT=g_codes[:, g_columns].bitcast(E5M2_X4),
+                        lhsT_scale=g_scales[:, g_columns],
+                        rhs=w_codes[:, w_columns].bitcast(E4M3_X4),
+                        rhs_scale=w_scales[:, w_columns],
+                        start=(c == 0),
+                        stop=(c == PASSES - 1),
+                    )
+                nc.vector.tensor_scalar_mul(
+                    out=result[:, t, :],
+                    in0=acc[:, place * CIN : (place + 1) * CIN],
+                    scalar1=factor[:, degree : degree + 1],
+                )
+            nc.sync.dma_start(
+                out=out[
+                    node_group * P : (node_group + 1) * P,
+                    row_group * TILES : (row_group + 1) * TILES,
+                    :,
+                ],
+                in_=result[:],
+            )
+
+        quantise_weights(0)
+        ahead = quantise_grad(0)
+        for chunk in range(1, W_CHUNKS):
+            quantise_weights(chunk)
+        for chunk in range(G_CHUNKS):
+            current = ahead
+            if chunk + 1 < G_CHUNKS:
+                ahead = quantise_grad(chunk + 1)
+            multiply(chunk, current[0], current[1])

@@ -26,6 +26,8 @@ NODE_GROUPS = NODES // P
 ROW_GROUPS = ROWS // TILES
 G_CHUNKS = NODE_GROUPS * ROW_GROUPS
 N_MOVING = DEGREES_PER_W_CHUNK * CIN
+LOADS_AHEAD = 4
+STORE_TILES = 2
 
 FLOPS = 2 * NODES * ROWS * CIN * K
 BYTES = 2 * NODES * ROWS * K + 2 * DEGREES * CIN * K + 2 * DEGREES + 4 * NODES * ROWS * CIN
@@ -40,38 +42,12 @@ def tile_linear_pa_kernel(tc, x, weights, path_weights, grad_out, out):
     with ExitStack() as ctx:
         ctx.enter_context(tc.manual_schedule())
         const = ctx.enter_context(tc.tile_pool(name="const", bufs=1))
-        raw_pool = ctx.enter_context(tc.tile_pool(name="raw", bufs=W_CHUNKS + G_CHUNKS))
+        raw_pool = ctx.enter_context(tc.tile_pool(name="raw", bufs=(W_CHUNKS + G_CHUNKS) * TILES))
         grouped_pool = ctx.enter_context(tc.tile_pool(name="grouped", bufs=2))
         codes_pool = ctx.enter_context(tc.tile_pool(name="codes", bufs=2))
-        result_pool = ctx.enter_context(tc.tile_pool(name="result", bufs=6))
+        result_pool = ctx.enter_context(tc.tile_pool(name="result", bufs=3))
         words_psum = ctx.enter_context(tc.psum_pool(name="words_psum", bufs=TILES))
         acc_psum = ctx.enter_context(tc.psum_pool(name="acc_psum", bufs=TILES))
-
-        def load_weights(chunk):
-            raw = raw_pool.tile([P, TILES * K], BF16, name="raw")
-            w_rows = weights.rearrange("l c k -> (l c) k")[chunk * TILES * P : (chunk + 1) * TILES * P, :]
-            nc.sync.dma_start(
-                out=raw[:].rearrange("p (t k) -> p t k", t=TILES),
-                in_=w_rows.rearrange("(t p) k -> p t k", p=P),
-            )
-            return raw
-
-        def load_grad(chunk):
-            node_group, row_group = divmod(chunk, ROW_GROUPS)
-            raw = raw_pool.tile([P, TILES * K], BF16, name="raw")
-            nc.sync.dma_start(
-                out=raw[:],
-                in_=grad_out.rearrange("n m k -> n (m k)")[
-                    node_group * P : (node_group + 1) * P,
-                    row_group * TILES * K : (row_group + 1) * TILES * K,
-                ],
-            )
-            return raw
-
-        w_raw = [load_weights(0)]
-        g_raw = [load_grad(0)]
-        w_raw.extend(load_weights(chunk) for chunk in range(1, W_CHUNKS))
-        g_raw.extend(load_grad(chunk) for chunk in range(1, G_CHUNKS))
 
         identity = const.tile([P, P], F32)
         make_identity(nc, identity[:])
@@ -80,20 +56,54 @@ def tile_linear_pa_kernel(tc, x, weights, path_weights, grad_out, out):
         factor = const.tile([P, DEGREES], F32)
         nc.vector.tensor_copy(out=factor[:], in_=factor_bf16[:])
 
+        def load_weights(chunk):
+            w_rows = weights.rearrange("l c k -> (l c) k")
+            tiles = []
+            for t in range(TILES):
+                raw = raw_pool.tile([P, K], BF16)
+                first = (chunk * TILES + t) * P
+                nc.sync.dma_start(out=raw[:], in_=w_rows[first : first + P, :])
+                tiles.append(raw)
+            return tiles
+
+        def groups_of(chunk):
+            row_group, node_group = divmod(chunk, NODE_GROUPS)
+            return node_group, row_group
+
+        def load_grad(chunk):
+            node_group, row_group = groups_of(chunk)
+            g_rows = grad_out.rearrange("n m k -> n (m k)")
+            tiles = []
+            for t in range(TILES):
+                raw = raw_pool.tile([P, K], BF16)
+                row = row_group * TILES + t
+                nc.sync.dma_start(
+                    out=raw[:],
+                    in_=g_rows[node_group * P : (node_group + 1) * P, row * K : (row + 1) * K],
+                )
+                tiles.append(raw)
+            return tiles
+
+        w_raw = [load_weights(0)]
+        g_raw = []
+        for chunk in range(LOADS_AHEAD):
+            g_raw.append(load_grad(chunk))
+            if 0 < chunk < W_CHUNKS:
+                w_raw.append(load_weights(chunk))
+
         w_codes = const.tile([P, W_CHUNKS * CHUNK_WORDS], U32, align_bytes=64)
         w_scales = const.tile([P, W_CHUNKS * CHUNK_WORDS], U8, align_bytes=64)
 
-        def quantise_chunk(raw, codes, scales, x4):
-            raw_words = raw[:].bitcast(F32)
+        def quantise_chunk(raw_tiles, codes, scales, x4):
             grouped = grouped_pool.tile([P, 4 * CHUNK_WORDS], BF16, align_bytes=64)
             grouped_words = grouped[:].bitcast(F32).rearrange(
                 "q (c t r u) -> q c t r u", c=PASSES, t=TILES, u=2
             )
             for t in range(TILES):
+                raw_words = raw_tiles[t][:].bitcast(F32)
                 bank = words_psum.tile([P, QUARTERS, P], F32)
                 for h in range(QUARTERS):
-                    first = (t * QUARTERS + h) * P
-                    nc.tensor.transpose(bank[:, h, :], raw_words[:, first : first + P], identity[:])
+                    nc.tensor.transpose(bank[:, h, :], raw_words[:, h * P : (h + 1) * P], identity[:])
                 nc.scalar.copy(
                     out=grouped_words[:, :, t, :, :],
                     in_=bank[:].rearrange("q (c u) r -> q c r u", u=2),
@@ -111,11 +121,11 @@ def tile_linear_pa_kernel(tc, x, weights, path_weights, grad_out, out):
             return g_codes, g_scales
 
         def multiply(chunk, g_codes, g_scales):
-            node_group, row_group = divmod(chunk, ROW_GROUPS)
+            node_group, row_group = groups_of(chunk)
             result = result_pool.tile([P, TILES, CIN], F32)
             for t in range(TILES):
                 degree = DEGREE_OF_ROW[row_group * TILES + t]
-                w_chunk, place = divmod(degree, DEGREES_PER_W_CHUNK)
+                w_chunk, half = divmod(degree, DEGREES_PER_W_CHUNK)
                 acc = acc_psum.tile([P, N_MOVING], F32)
                 for c in range(PASSES):
                     g_columns = slice((c * TILES + t) * P, (c * TILES + t + 1) * P)
@@ -132,24 +142,28 @@ def tile_linear_pa_kernel(tc, x, weights, path_weights, grad_out, out):
                     )
                 nc.vector.tensor_scalar_mul(
                     out=result[:, t, :],
-                    in0=acc[:, place * CIN : (place + 1) * CIN],
+                    in0=acc[:, half * CIN : (half + 1) * CIN],
                     scalar1=factor[:, degree : degree + 1],
                 )
-            nc.sync.dma_start(
-                out=out[
-                    node_group * P : (node_group + 1) * P,
-                    row_group * TILES : (row_group + 1) * TILES,
-                    :,
-                ],
-                in_=result[:],
-            )
+                if (t + 1) % STORE_TILES == 0:
+                    oldest = t + 1 - STORE_TILES
+                    nc.sync.dma_start(
+                        out=out[
+                            node_group * P : (node_group + 1) * P,
+                            row_group * TILES + oldest : row_group * TILES + t + 1,
+                            :,
+                        ],
+                        in_=result[:, oldest : t + 1, :],
+                    )
 
         quantise_weights(0)
         ahead = quantise_grad(0)
-        for chunk in range(1, W_CHUNKS):
-            quantise_weights(chunk)
         for chunk in range(G_CHUNKS):
+            if chunk + LOADS_AHEAD < G_CHUNKS:
+                g_raw.append(load_grad(chunk + LOADS_AHEAD))
             current = ahead
             if chunk + 1 < G_CHUNKS:
                 ahead = quantise_grad(chunk + 1)
+            if 0 < chunk < W_CHUNKS:
+                quantise_weights(chunk)
             multiply(chunk, current[0], current[1])

@@ -18,16 +18,13 @@ DEGREE_OF_ROW = [l for l in range(DEGREES) for row in range(2 * l + 1)]
 K_PASS = 4 * P
 PASSES = K // K_PASS
 QUARTERS = K // 2 // P
-TILES = 4
+TILES = NODES // P
 CHUNK_WORDS = TILES * PASSES * P
 W_CHUNKS = DEGREES * CIN // (TILES * P)
-DEGREES_PER_W_CHUNK = DEGREES // W_CHUNKS
-NODE_GROUPS = NODES // P
-ROW_GROUPS = ROWS // TILES
-G_CHUNKS = NODE_GROUPS * ROW_GROUPS
-N_MOVING = DEGREES_PER_W_CHUNK * CIN
+CIN_HALVES = CIN // P
+PAIR = 2
+SCALAR_TILES = 3
 LOADS_AHEAD = 4
-STORE_TILES = 2
 
 FLOPS = 2 * NODES * ROWS * CIN * K
 BYTES = 2 * NODES * ROWS * K + 2 * DEGREES * CIN * K + 2 * DEGREES + 4 * NODES * ROWS * CIN
@@ -42,12 +39,14 @@ def tile_linear_pa_kernel(tc, x, weights, path_weights, grad_out, out):
     with ExitStack() as ctx:
         ctx.enter_context(tc.manual_schedule())
         const = ctx.enter_context(tc.tile_pool(name="const", bufs=1))
-        raw_pool = ctx.enter_context(tc.tile_pool(name="raw", bufs=(W_CHUNKS + G_CHUNKS) * TILES))
+        raw_pool = ctx.enter_context(tc.tile_pool(name="raw", bufs=(W_CHUNKS + ROWS) * TILES))
         grouped_pool = ctx.enter_context(tc.tile_pool(name="grouped", bufs=2))
         codes_pool = ctx.enter_context(tc.tile_pool(name="codes", bufs=2))
-        result_pool = ctx.enter_context(tc.tile_pool(name="result", bufs=3))
+        product_pool = ctx.enter_context(tc.tile_pool(name="product", bufs=2 * CIN_HALVES))
+        result_pool = ctx.enter_context(tc.tile_pool(name="result", bufs=4))
         words_psum = ctx.enter_context(tc.psum_pool(name="words_psum", bufs=TILES))
-        acc_psum = ctx.enter_context(tc.psum_pool(name="acc_psum", bufs=TILES))
+        acc_psum = ctx.enter_context(tc.psum_pool(name="acc_psum", bufs=CIN_HALVES))
+        back_psum = ctx.enter_context(tc.psum_pool(name="back_psum", bufs=TILES // PAIR))
 
         identity = const.tile([P, P], F32)
         make_identity(nc, identity[:])
@@ -66,35 +65,26 @@ def tile_linear_pa_kernel(tc, x, weights, path_weights, grad_out, out):
                 tiles.append(raw)
             return tiles
 
-        def groups_of(chunk):
-            row_group, node_group = divmod(chunk, NODE_GROUPS)
-            return node_group, row_group
-
-        def load_grad(chunk):
-            node_group, row_group = groups_of(chunk)
+        def load_grad(m):
             g_rows = grad_out.rearrange("n m k -> n (m k)")
             tiles = []
             for t in range(TILES):
                 raw = raw_pool.tile([P, K], BF16)
-                row = row_group * TILES + t
-                nc.sync.dma_start(
-                    out=raw[:],
-                    in_=g_rows[node_group * P : (node_group + 1) * P, row * K : (row + 1) * K],
-                )
+                nc.sync.dma_start(out=raw[:], in_=g_rows[t * P : (t + 1) * P, m * K : (m + 1) * K])
                 tiles.append(raw)
             return tiles
 
         w_raw = [load_weights(0)]
         g_raw = []
-        for chunk in range(LOADS_AHEAD):
-            g_raw.append(load_grad(chunk))
-            if 0 < chunk < W_CHUNKS:
-                w_raw.append(load_weights(chunk))
+        for m in range(LOADS_AHEAD):
+            g_raw.append(load_grad(m))
+            if 0 < m < W_CHUNKS:
+                w_raw.append(load_weights(m))
 
         w_codes = const.tile([P, W_CHUNKS * CHUNK_WORDS], U32, align_bytes=64)
         w_scales = const.tile([P, W_CHUNKS * CHUNK_WORDS], U8, align_bytes=64)
 
-        def quantise_chunk(raw_tiles, codes, scales, x4):
+        def transpose_chunk(raw_tiles):
             grouped = grouped_pool.tile([P, 4 * CHUNK_WORDS], BF16, align_bytes=64)
             grouped_words = grouped[:].bitcast(F32).rearrange(
                 "q (c t r u) -> q c t r u", c=PASSES, t=TILES, u=2
@@ -104,66 +94,85 @@ def tile_linear_pa_kernel(tc, x, weights, path_weights, grad_out, out):
                 bank = words_psum.tile([P, QUARTERS, P], F32)
                 for h in range(QUARTERS):
                     nc.tensor.transpose(bank[:, h, :], raw_words[:, h * P : (h + 1) * P], identity[:])
-                nc.scalar.copy(
-                    out=grouped_words[:, :, t, :, :],
-                    in_=bank[:].rearrange("q (c u) r -> q c r u", u=2),
-                )
-            nc.vector.quantize_mx(out=codes.bitcast(x4), scales=scales, in_=grouped[:])
+                paired = bank[:].rearrange("q (c u) r -> q c r u", u=2)
+                if t < SCALAR_TILES:
+                    nc.scalar.copy(out=grouped_words[:, :, t, :, :], in_=paired)
+                else:
+                    nc.vector.tensor_copy(out=grouped_words[:, :, t, :, :], in_=paired)
+            return grouped
 
         def quantise_weights(chunk):
             columns = slice(chunk * CHUNK_WORDS, (chunk + 1) * CHUNK_WORDS)
-            quantise_chunk(w_raw[chunk], w_codes[:, columns], w_scales[:, columns], E4M3_X4)
+            grouped = transpose_chunk(w_raw[chunk])
+            nc.vector.quantize_mx(
+                out=w_codes[:, columns].bitcast(E4M3_X4), scales=w_scales[:, columns], in_=grouped[:]
+            )
 
-        def quantise_grad(chunk):
+        def quantise_grad(grouped):
             g_codes = codes_pool.tile([P, CHUNK_WORDS], U32, align_bytes=64)
             g_scales = codes_pool.tile([P, CHUNK_WORDS], U8, align_bytes=64)
-            quantise_chunk(g_raw[chunk], g_codes[:], g_scales[:], E5M2_X4)
+            nc.vector.quantize_mx(out=g_codes[:].bitcast(E5M2_X4), scales=g_scales[:], in_=grouped[:])
             return g_codes, g_scales
 
-        def multiply(chunk, g_codes, g_scales):
-            node_group, row_group = groups_of(chunk)
-            result = result_pool.tile([P, TILES, CIN], F32)
-            for t in range(TILES):
-                degree = DEGREE_OF_ROW[row_group * TILES + t]
-                w_chunk, half = divmod(degree, DEGREES_PER_W_CHUNK)
-                acc = acc_psum.tile([P, N_MOVING], F32)
+        def multiply(m, g_codes, g_scales):
+            degree = DEGREE_OF_ROW[m]
+            products = []
+            for half in range(CIN_HALVES):
+                w_chunk, w_tile = divmod(degree * CIN_HALVES + half, TILES)
+                acc = acc_psum.tile([P, NODES], F32)
                 for c in range(PASSES):
-                    g_columns = slice((c * TILES + t) * P, (c * TILES + t + 1) * P)
-                    w_first = w_chunk * CHUNK_WORDS + c * N_MOVING
-                    w_columns = slice(w_first, w_first + N_MOVING)
+                    w_first = w_chunk * CHUNK_WORDS + (c * TILES + w_tile) * P
+                    w_columns = slice(w_first, w_first + P)
+                    g_columns = slice(c * NODES, (c + 1) * NODES)
                     nc.tensor.matmul_mx(
                         out=acc[:],
-                        lhsT=g_codes[:, g_columns].bitcast(E5M2_X4),
-                        lhsT_scale=g_scales[:, g_columns],
-                        rhs=w_codes[:, w_columns].bitcast(E4M3_X4),
-                        rhs_scale=w_scales[:, w_columns],
+                        lhsT=w_codes[:, w_columns].bitcast(E4M3_X4),
+                        lhsT_scale=w_scales[:, w_columns],
+                        rhs=g_codes[:, g_columns].bitcast(E5M2_X4),
+                        rhs_scale=g_scales[:, g_columns],
                         start=(c == 0),
                         stop=(c == PASSES - 1),
                     )
+                product = product_pool.tile([P, NODES], F32)
+                nc.scalar.copy(out=product[:], in_=acc[:])
+                products.append(product)
+            return products
+
+        def store_row(m, products):
+            degree = DEGREE_OF_ROW[m]
+            out_tiles = out.rearrange("(t p) m c -> p t m c", p=P)
+            for pair in range(TILES // PAIR):
+                back = back_psum.tile([P, PAIR, CIN_HALVES, P], F32)
+                for i in range(PAIR):
+                    t = pair * PAIR + i
+                    for half in range(CIN_HALVES):
+                        nc.tensor.transpose(
+                            back[:, i, half, :], products[half][:, t * P : (t + 1) * P], identity[:]
+                        )
+                result = result_pool.tile([P, PAIR, CIN], F32)
                 nc.vector.tensor_scalar_mul(
-                    out=result[:, t, :],
-                    in0=acc[:, half * CIN : (half + 1) * CIN],
+                    out=result[:],
+                    in0=back[:].rearrange("p i h c -> p i (h c)"),
                     scalar1=factor[:, degree : degree + 1],
                 )
-                if (t + 1) % STORE_TILES == 0:
-                    oldest = t + 1 - STORE_TILES
-                    nc.sync.dma_start(
-                        out=out[
-                            node_group * P : (node_group + 1) * P,
-                            row_group * TILES + oldest : row_group * TILES + t + 1,
-                            :,
-                        ],
-                        in_=result[:, oldest : t + 1, :],
-                    )
+                nc.sync.dma_start(
+                    out=out_tiles[:, pair * PAIR : (pair + 1) * PAIR, m, :], in_=result[:]
+                )
 
         quantise_weights(0)
-        ahead = quantise_grad(0)
-        for chunk in range(G_CHUNKS):
-            if chunk + LOADS_AHEAD < G_CHUNKS:
-                g_raw.append(load_grad(chunk + LOADS_AHEAD))
+        ahead = quantise_grad(transpose_chunk(g_raw[0]))
+        products = []
+        for m in range(ROWS):
+            if m + LOADS_AHEAD < ROWS:
+                g_raw.append(load_grad(m + LOADS_AHEAD))
             current = ahead
-            if chunk + 1 < G_CHUNKS:
-                ahead = quantise_grad(chunk + 1)
-            if 0 < chunk < W_CHUNKS:
-                quantise_weights(chunk)
-            multiply(chunk, current[0], current[1])
+            if m + 1 < ROWS:
+                grouped_ahead = transpose_chunk(g_raw[m + 1])
+            if 0 < m < W_CHUNKS:
+                quantise_weights(m)
+            if m > 0:
+                store_row(m - 1, products)
+            if m + 1 < ROWS:
+                ahead = quantise_grad(grouped_ahead)
+            products = multiply(m, current[0], current[1])
+        store_row(ROWS - 1, products)

@@ -13,7 +13,8 @@ E5M2_X4 = mybir.dt.float8_e5m2_x4
 P = 128
 NODES, DEGREES, CIN, K = 512, 4, 256, 1024
 ROWS = DEGREES * DEGREES
-DEGREE_OF_ROW = [l for l in range(DEGREES) for row in range(2 * l + 1)]
+G_CHUNKS = ROWS
+DEGREE_OF_CHUNK = [l for l in range(DEGREES) for chunk in range(2 * l + 1)]
 
 K_PASS = 4 * P
 PASSES = K // K_PASS
@@ -39,11 +40,11 @@ def tile_linear_pa_kernel(tc, x, weights, path_weights, grad_out, out):
     with ExitStack() as ctx:
         ctx.enter_context(tc.manual_schedule())
         const = ctx.enter_context(tc.tile_pool(name="const", bufs=1))
-        raw_pool = ctx.enter_context(tc.tile_pool(name="raw", bufs=(W_CHUNKS + ROWS) * TILES))
+        raw_pool = ctx.enter_context(tc.tile_pool(name="raw", bufs=W_CHUNKS + G_CHUNKS))
         grouped_pool = ctx.enter_context(tc.tile_pool(name="grouped", bufs=2))
         codes_pool = ctx.enter_context(tc.tile_pool(name="codes", bufs=2))
         product_pool = ctx.enter_context(tc.tile_pool(name="product", bufs=2 * CIN_HALVES))
-        result_pool = ctx.enter_context(tc.tile_pool(name="result", bufs=4))
+        result_pool = ctx.enter_context(tc.tile_pool(name="result", bufs=3))
         words_psum = ctx.enter_context(tc.psum_pool(name="words_psum", bufs=TILES))
         acc_psum = ctx.enter_context(tc.psum_pool(name="acc_psum", bufs=CIN_HALVES))
         back_psum = ctx.enter_context(tc.psum_pool(name="back_psum", bufs=TILES // PAIR))
@@ -57,43 +58,56 @@ def tile_linear_pa_kernel(tc, x, weights, path_weights, grad_out, out):
 
         def load_weights(chunk):
             w_rows = weights.rearrange("l c k -> (l c) k")
-            tiles = []
+            raw = raw_pool.tile([P, TILES * K], BF16)
             for t in range(TILES):
-                raw = raw_pool.tile([P, K], BF16)
                 first = (chunk * TILES + t) * P
-                nc.sync.dma_start(out=raw[:], in_=w_rows[first : first + P, :])
-                tiles.append(raw)
-            return tiles
+                nc.sync.dma_start(out=raw[:, t * K : (t + 1) * K], in_=w_rows[first : first + P, :])
+            return raw
 
-        def load_grad(m):
+        def segments_of(chunk):
+            degree = DEGREE_OF_CHUNK[chunk]
+            width = 2 * degree + 1
+            number = (chunk - degree * degree) * TILES
+            segments = []
+            t = 0
+            while t < TILES:
+                node_tile, row = divmod(number + t, width)
+                rows = min(TILES - t, width - row)
+                segments.append((t, node_tile, degree * degree + row, rows))
+                t += rows
+            return segments
+
+        def load_grad(chunk):
             g_rows = grad_out.rearrange("n m k -> n (m k)")
-            tiles = []
-            for t in range(TILES):
-                raw = raw_pool.tile([P, K], BF16)
-                nc.sync.dma_start(out=raw[:], in_=g_rows[t * P : (t + 1) * P, m * K : (m + 1) * K])
-                tiles.append(raw)
-            return tiles
+            raw = raw_pool.tile([P, TILES * K], BF16)
+            for t, node_tile, m, rows in segments_of(chunk):
+                nc.sync.dma_start(
+                    out=raw[:, t * K : (t + rows) * K],
+                    in_=g_rows[node_tile * P : (node_tile + 1) * P, m * K : (m + rows) * K],
+                )
+            return raw
 
         w_raw = [load_weights(0)]
         g_raw = []
-        for m in range(LOADS_AHEAD):
-            g_raw.append(load_grad(m))
-            if 0 < m < W_CHUNKS:
-                w_raw.append(load_weights(m))
+        for chunk in range(LOADS_AHEAD):
+            g_raw.append(load_grad(chunk))
+            if 0 < chunk < W_CHUNKS:
+                w_raw.append(load_weights(chunk))
 
         w_codes = const.tile([P, W_CHUNKS * CHUNK_WORDS], U32, align_bytes=64)
         w_scales = const.tile([P, W_CHUNKS * CHUNK_WORDS], U8, align_bytes=64)
 
-        def transpose_chunk(raw_tiles):
+        def transpose_chunk(raw):
             grouped = grouped_pool.tile([P, 4 * CHUNK_WORDS], BF16, align_bytes=64)
             grouped_words = grouped[:].bitcast(F32).rearrange(
                 "q (c t r u) -> q c t r u", c=PASSES, t=TILES, u=2
             )
+            raw_words = raw[:].bitcast(F32)
             for t in range(TILES):
-                raw_words = raw_tiles[t][:].bitcast(F32)
                 bank = words_psum.tile([P, QUARTERS, P], F32)
                 for h in range(QUARTERS):
-                    nc.tensor.transpose(bank[:, h, :], raw_words[:, h * P : (h + 1) * P], identity[:])
+                    first = (t * QUARTERS + h) * P
+                    nc.tensor.transpose(bank[:, h, :], raw_words[:, first : first + P], identity[:])
                 paired = bank[:].rearrange("q (c u) r -> q c r u", u=2)
                 if t < SCALAR_TILES:
                     nc.scalar.copy(out=grouped_words[:, :, t, :, :], in_=paired)
@@ -114,16 +128,16 @@ def tile_linear_pa_kernel(tc, x, weights, path_weights, grad_out, out):
             nc.vector.quantize_mx(out=g_codes[:].bitcast(E5M2_X4), scales=g_scales[:], in_=grouped[:])
             return g_codes, g_scales
 
-        def multiply(m, g_codes, g_scales):
-            degree = DEGREE_OF_ROW[m]
+        def multiply(chunk, g_codes, g_scales):
+            degree = DEGREE_OF_CHUNK[chunk]
             products = []
             for half in range(CIN_HALVES):
                 w_chunk, w_tile = divmod(degree * CIN_HALVES + half, TILES)
-                acc = acc_psum.tile([P, NODES], F32)
+                acc = acc_psum.tile([P, TILES * P], F32)
                 for c in range(PASSES):
                     w_first = w_chunk * CHUNK_WORDS + (c * TILES + w_tile) * P
                     w_columns = slice(w_first, w_first + P)
-                    g_columns = slice(c * NODES, (c + 1) * NODES)
+                    g_columns = slice(c * TILES * P, (c + 1) * TILES * P)
                     nc.tensor.matmul_mx(
                         out=acc[:],
                         lhsT=w_codes[:, w_columns].bitcast(E4M3_X4),
@@ -133,14 +147,14 @@ def tile_linear_pa_kernel(tc, x, weights, path_weights, grad_out, out):
                         start=(c == 0),
                         stop=(c == PASSES - 1),
                     )
-                product = product_pool.tile([P, NODES], F32)
+                product = product_pool.tile([P, TILES * P], F32)
                 nc.scalar.copy(out=product[:], in_=acc[:])
                 products.append(product)
             return products
 
-        def store_row(m, products):
-            degree = DEGREE_OF_ROW[m]
-            out_tiles = out.rearrange("(t p) m c -> p t m c", p=P)
+        def store_chunk(chunk, products):
+            degree = DEGREE_OF_CHUNK[chunk]
+            result = result_pool.tile([P, TILES * CIN], F32)
             for pair in range(TILES // PAIR):
                 back = back_psum.tile([P, PAIR, CIN_HALVES, P], F32)
                 for i in range(PAIR):
@@ -149,30 +163,32 @@ def tile_linear_pa_kernel(tc, x, weights, path_weights, grad_out, out):
                         nc.tensor.transpose(
                             back[:, i, half, :], products[half][:, t * P : (t + 1) * P], identity[:]
                         )
-                result = result_pool.tile([P, PAIR, CIN], F32)
                 nc.vector.tensor_scalar_mul(
-                    out=result[:],
-                    in0=back[:].rearrange("p i h c -> p i (h c)"),
+                    out=result[:, pair * PAIR * CIN : (pair + 1) * PAIR * CIN],
+                    in0=back[:].rearrange("p i h c -> p (i h c)"),
                     scalar1=factor[:, degree : degree + 1],
                 )
+            out_rows = out.rearrange("n m c -> n (m c)")
+            for t, node_tile, m, rows in segments_of(chunk):
                 nc.sync.dma_start(
-                    out=out_tiles[:, pair * PAIR : (pair + 1) * PAIR, m, :], in_=result[:]
+                    out=out_rows[node_tile * P : (node_tile + 1) * P, m * CIN : (m + rows) * CIN],
+                    in_=result[:, t * CIN : (t + rows) * CIN],
                 )
 
         quantise_weights(0)
         ahead = quantise_grad(transpose_chunk(g_raw[0]))
         products = []
-        for m in range(ROWS):
-            if m + LOADS_AHEAD < ROWS:
-                g_raw.append(load_grad(m + LOADS_AHEAD))
+        for chunk in range(G_CHUNKS):
+            if chunk + LOADS_AHEAD < G_CHUNKS:
+                g_raw.append(load_grad(chunk + LOADS_AHEAD))
             current = ahead
-            if m + 1 < ROWS:
-                grouped_ahead = transpose_chunk(g_raw[m + 1])
-            if 0 < m < W_CHUNKS:
-                quantise_weights(m)
-            if m > 0:
-                store_row(m - 1, products)
-            if m + 1 < ROWS:
+            if chunk + 1 < G_CHUNKS:
+                grouped_ahead = transpose_chunk(g_raw[chunk + 1])
+            if 0 < chunk < W_CHUNKS:
+                quantise_weights(chunk)
+            if chunk > 0:
+                store_chunk(chunk - 1, products)
+            if chunk + 1 < G_CHUNKS:
                 ahead = quantise_grad(grouped_ahead)
-            products = multiply(m, current[0], current[1])
-        store_row(ROWS - 1, products)
+            products = multiply(chunk, current[0], current[1])
+        store_chunk(G_CHUNKS - 1, products)

@@ -20,8 +20,6 @@ K_PASS = 4 * P
 PASSES = K // K_PASS
 QUARTERS = K // 2 // P
 TILES = NODES // P
-CHUNK_WORDS = TILES * PASSES * P
-W_CHUNKS = DEGREES * CIN // (TILES * P)
 CIN_HALVES = CIN // P
 PAIR = 2
 SCALAR_TILES = 3
@@ -40,7 +38,8 @@ def tile_linear_pa_kernel(tc, x, weights, path_weights, grad_out, out):
     with ExitStack() as ctx:
         ctx.enter_context(tc.manual_schedule())
         const = ctx.enter_context(tc.tile_pool(name="const", bufs=1))
-        raw_pool = ctx.enter_context(tc.tile_pool(name="raw", bufs=W_CHUNKS + G_CHUNKS))
+        raw_pool = ctx.enter_context(tc.tile_pool(name="raw", bufs=G_CHUNKS))
+        w_raw_pool = ctx.enter_context(tc.tile_pool(name="w_raw", bufs=DEGREES))
         grouped_pool = ctx.enter_context(tc.tile_pool(name="grouped", bufs=2))
         codes_pool = ctx.enter_context(tc.tile_pool(name="codes", bufs=2))
         product_pool = ctx.enter_context(tc.tile_pool(name="product", bufs=2 * CIN_HALVES))
@@ -56,13 +55,14 @@ def tile_linear_pa_kernel(tc, x, weights, path_weights, grad_out, out):
         factor = const.tile([P, DEGREES], F32)
         nc.vector.tensor_copy(out=factor[:], in_=factor_bf16[:])
 
-        def load_weights(chunk):
-            w_rows = weights.rearrange("l c k -> (l c) k")
-            raw = raw_pool.tile([P, TILES * K], BF16)
-            for t in range(TILES):
-                first = (chunk * TILES + t) * P
-                nc.sync.dma_start(out=raw[:, t * K : (t + 1) * K], in_=w_rows[first : first + P, :])
-            return raw
+        def load_weights(degree):
+            w_raw = w_raw_pool.tile([P, CIN_HALVES * K], BF16)
+            for half in range(CIN_HALVES):
+                nc.sync.dma_start(
+                    out=w_raw[:, half * K : (half + 1) * K],
+                    in_=weights[degree, half * P : (half + 1) * P, :],
+                )
+            return w_raw
 
         def segments_of(chunk):
             degree = DEGREE_OF_CHUNK[chunk]
@@ -87,23 +87,31 @@ def tile_linear_pa_kernel(tc, x, weights, path_weights, grad_out, out):
                 )
             return raw
 
-        w_raw = [load_weights(0)]
-        g_raw = []
+        def is_first_of_degree(chunk):
+            return chunk == DEGREE_OF_CHUNK[chunk] * DEGREE_OF_CHUNK[chunk]
+
+        raw_of_chunk = []
+        raw_of_degree = [load_weights(0)]
+
+        def load_next_chunk():
+            chunk = len(raw_of_chunk)
+            raw_of_chunk.append(load_grad(chunk))
+            if chunk > 0 and is_first_of_degree(chunk):
+                raw_of_degree.append(load_weights(DEGREE_OF_CHUNK[chunk]))
+
         for chunk in range(LOADS_AHEAD):
-            g_raw.append(load_grad(chunk))
-            if 0 < chunk < W_CHUNKS:
-                w_raw.append(load_weights(chunk))
+            load_next_chunk()
 
-        w_codes = const.tile([P, W_CHUNKS * CHUNK_WORDS], U32, align_bytes=64)
-        w_scales = const.tile([P, W_CHUNKS * CHUNK_WORDS], U8, align_bytes=64)
+        w_codes = const.tile([P, DEGREES * PASSES * CIN], U32, align_bytes=64)
+        w_scales = const.tile([P, DEGREES * PASSES * CIN], U8, align_bytes=64)
 
-        def transpose_chunk(raw):
-            grouped = grouped_pool.tile([P, 4 * CHUNK_WORDS], BF16, align_bytes=64)
+        def transpose_tiles(raw, tiles):
+            grouped = grouped_pool.tile([P, tiles * K], BF16, align_bytes=64)
             grouped_words = grouped[:].bitcast(F32).rearrange(
-                "q (c t r u) -> q c t r u", c=PASSES, t=TILES, u=2
+                "q (c t r u) -> q c t r u", c=PASSES, t=tiles, u=2
             )
             raw_words = raw[:].bitcast(F32)
-            for t in range(TILES):
+            for t in range(tiles):
                 bank = words_psum.tile([P, QUARTERS, P], F32)
                 for h in range(QUARTERS):
                     first = (t * QUARTERS + h) * P
@@ -115,16 +123,16 @@ def tile_linear_pa_kernel(tc, x, weights, path_weights, grad_out, out):
                     nc.vector.tensor_copy(out=grouped_words[:, :, t, :, :], in_=paired)
             return grouped
 
-        def quantise_weights(chunk):
-            columns = slice(chunk * CHUNK_WORDS, (chunk + 1) * CHUNK_WORDS)
-            grouped = transpose_chunk(w_raw[chunk])
+        def quantise_weights(degree):
+            columns = slice(degree * PASSES * CIN, (degree + 1) * PASSES * CIN)
+            grouped = transpose_tiles(raw_of_degree[degree], CIN_HALVES)
             nc.vector.quantize_mx(
                 out=w_codes[:, columns].bitcast(E4M3_X4), scales=w_scales[:, columns], in_=grouped[:]
             )
 
         def quantise_grad(grouped):
-            g_codes = codes_pool.tile([P, CHUNK_WORDS], U32, align_bytes=64)
-            g_scales = codes_pool.tile([P, CHUNK_WORDS], U8, align_bytes=64)
+            g_codes = codes_pool.tile([P, PASSES * TILES * P], U32, align_bytes=64)
+            g_scales = codes_pool.tile([P, PASSES * TILES * P], U8, align_bytes=64)
             nc.vector.quantize_mx(out=g_codes[:].bitcast(E5M2_X4), scales=g_scales[:], in_=grouped[:])
             return g_codes, g_scales
 
@@ -132,10 +140,9 @@ def tile_linear_pa_kernel(tc, x, weights, path_weights, grad_out, out):
             degree = DEGREE_OF_CHUNK[chunk]
             products = []
             for half in range(CIN_HALVES):
-                w_chunk, w_tile = divmod(degree * CIN_HALVES + half, TILES)
                 acc = acc_psum.tile([P, TILES * P], F32)
                 for c in range(PASSES):
-                    w_first = w_chunk * CHUNK_WORDS + (c * TILES + w_tile) * P
+                    w_first = (degree * PASSES + c) * CIN + half * P
                     w_columns = slice(w_first, w_first + P)
                     g_columns = slice(c * TILES * P, (c + 1) * TILES * P)
                     nc.tensor.matmul_mx(
@@ -176,16 +183,16 @@ def tile_linear_pa_kernel(tc, x, weights, path_weights, grad_out, out):
                 )
 
         quantise_weights(0)
-        ahead = quantise_grad(transpose_chunk(g_raw[0]))
+        ahead = quantise_grad(transpose_tiles(raw_of_chunk[0], TILES))
         products = []
         for chunk in range(G_CHUNKS):
-            if chunk + LOADS_AHEAD < G_CHUNKS:
-                g_raw.append(load_grad(chunk + LOADS_AHEAD))
+            if len(raw_of_chunk) < G_CHUNKS:
+                load_next_chunk()
             current = ahead
+            if chunk > 0 and is_first_of_degree(chunk):
+                quantise_weights(DEGREE_OF_CHUNK[chunk])
             if chunk + 1 < G_CHUNKS:
-                grouped_ahead = transpose_chunk(g_raw[chunk + 1])
-            if 0 < chunk < W_CHUNKS:
-                quantise_weights(chunk)
+                grouped_ahead = transpose_tiles(raw_of_chunk[chunk + 1], TILES)
             if chunk > 0:
                 store_chunk(chunk - 1, products)
             if chunk + 1 < G_CHUNKS:

@@ -23,7 +23,7 @@ TILES = NODES // P
 CIN_HALVES = CIN // P
 PAIR = 2
 SCALAR_TILES = 3
-LOADS_AHEAD = 4
+LOADS_AHEAD = G_CHUNKS
 
 FLOPS = 2 * NODES * ROWS * CIN * K
 BYTES = 2 * NODES * ROWS * K + 2 * DEGREES * CIN * K + 2 * DEGREES + 4 * NODES * ROWS * CIN
@@ -43,7 +43,6 @@ def tile_linear_pa_kernel(tc, x, weights, path_weights, grad_out, out):
         grouped_pool = ctx.enter_context(tc.tile_pool(name="grouped", bufs=2))
         codes_pool = ctx.enter_context(tc.tile_pool(name="codes", bufs=2))
         product_pool = ctx.enter_context(tc.tile_pool(name="product", bufs=2 * CIN_HALVES))
-        result_pool = ctx.enter_context(tc.tile_pool(name="result", bufs=3))
         words_psum = ctx.enter_context(tc.psum_pool(name="words_psum", bufs=TILES))
         acc_psum = ctx.enter_context(tc.psum_pool(name="acc_psum", bufs=CIN_HALVES))
         back_psum = ctx.enter_context(tc.psum_pool(name="back_psum", bufs=TILES // PAIR))
@@ -79,7 +78,7 @@ def tile_linear_pa_kernel(tc, x, weights, path_weights, grad_out, out):
 
         def load_grad(chunk):
             g_rows = grad_out.rearrange("n m k -> n (m k)")
-            raw = raw_pool.tile([P, TILES * K], BF16)
+            raw = raw_pool.tile([P, TILES * K], BF16, tag="raw")
             for t, node_tile, m, rows in segments_of(chunk):
                 nc.sync.dma_start(
                     out=raw[:, t * K : (t + rows) * K],
@@ -161,7 +160,7 @@ def tile_linear_pa_kernel(tc, x, weights, path_weights, grad_out, out):
 
         def store_chunk(chunk, products):
             degree = DEGREE_OF_CHUNK[chunk]
-            result = result_pool.tile([P, TILES * CIN], F32)
+            result = raw_pool.tile([P, TILES * CIN], F32, tag="raw")
             for pair in range(TILES // PAIR):
                 back = back_psum.tile([P, PAIR, CIN_HALVES, P], F32)
                 for i in range(PAIR):

@@ -23,6 +23,7 @@ TILES = NODES // P
 CIN_HALVES = CIN // P
 PAIR = 2
 SCALAR_TILES = 3
+RAW_BYTES = 2 * TILES * K
 LOADS_AHEAD = G_CHUNKS
 
 FLOPS = 2 * NODES * ROWS * CIN * K
@@ -38,7 +39,7 @@ def tile_linear_pa_kernel(tc, x, weights, path_weights, grad_out, out):
     with ExitStack() as ctx:
         ctx.enter_context(tc.manual_schedule())
         const = ctx.enter_context(tc.tile_pool(name="const", bufs=1))
-        raw_pool = ctx.enter_context(tc.tile_pool(name="raw", bufs=G_CHUNKS))
+        raw_pool = ctx.enter_context(tc.tile_pool(name="raw", bufs=1))
         w_raw_pool = ctx.enter_context(tc.tile_pool(name="w_raw", bufs=DEGREES))
         grouped_pool = ctx.enter_context(tc.tile_pool(name="grouped", bufs=2))
         codes_pool = ctx.enter_context(tc.tile_pool(name="codes", bufs=2))
@@ -78,7 +79,7 @@ def tile_linear_pa_kernel(tc, x, weights, path_weights, grad_out, out):
 
         def load_grad(chunk):
             g_rows = grad_out.rearrange("n m k -> n (m k)")
-            raw = raw_pool.tile([P, TILES * K], BF16, tag="raw")
+            raw = raw_pool.tile([P, TILES * K], BF16, name="raw%d" % chunk, offset=chunk * RAW_BYTES)
             for t, node_tile, m, rows in segments_of(chunk):
                 nc.sync.dma_start(
                     out=raw[:, t * K : (t + rows) * K],
@@ -160,7 +161,7 @@ def tile_linear_pa_kernel(tc, x, weights, path_weights, grad_out, out):
 
         def store_chunk(chunk, products):
             degree = DEGREE_OF_CHUNK[chunk]
-            result = raw_pool.tile([P, TILES * CIN], F32, tag="raw")
+            result = raw_pool.tile([P, TILES * CIN], F32, name="result%d" % chunk, offset=chunk * RAW_BYTES)
             for pair in range(TILES // PAIR):
                 back = back_psum.tile([P, PAIR, CIN_HALVES, P], F32)
                 for i in range(PAIR):

@@ -14,7 +14,9 @@ P = 128
 NODES, DEGREES, CIN, K = 512, 4, 256, 1024
 ROWS = DEGREES * DEGREES
 G_CHUNKS = ROWS
-DEGREE_OF_CHUNK = [l for l in range(DEGREES) for chunk in range(2 * l + 1)]
+DEGREE_ORDER = [3, 2, 1, 0]
+DEGREE_OF_CHUNK = [l for l in DEGREE_ORDER for chunk in range(2 * l + 1)]
+FIRST_CHUNK = [DEGREE_OF_CHUNK.index(l) for l in range(DEGREES)]
 
 K_PASS = 4 * P
 PASSES = K // K_PASS
@@ -23,6 +25,8 @@ TILES = NODES // P
 CIN_HALVES = CIN // P
 PAIR = 2
 SCALAR_TILES = 3
+WARM_UP_MATMULS = 5
+FINE_LOADS = 2
 RAW_BYTES = 2 * TILES * K
 LOADS_AHEAD = G_CHUNKS
 
@@ -48,6 +52,12 @@ def tile_linear_pa_kernel(tc, x, weights, path_weights, grad_out, out):
         acc_psum = ctx.enter_context(tc.psum_pool(name="acc_psum", bufs=CIN_HALVES))
         back_psum = ctx.enter_context(tc.psum_pool(name="back_psum", bufs=TILES // PAIR))
 
+        zeros = const.tile([P, TILES * P], BF16)
+        nc.vector.memset(zeros[:], 0.0)
+        for i in range(WARM_UP_MATMULS):
+            unread = acc_psum.tile([P, TILES * P], F32, tag="acc")
+            nc.tensor.matmul(out=unread[:], lhsT=zeros[:, :P], rhs=zeros[:], start=True, stop=True)
+
         identity = const.tile([P, P], F32)
         make_identity(nc, identity[:])
         factor_bf16 = const.tile([P, DEGREES], BF16)
@@ -67,7 +77,7 @@ def tile_linear_pa_kernel(tc, x, weights, path_weights, grad_out, out):
         def segments_of(chunk):
             degree = DEGREE_OF_CHUNK[chunk]
             width = 2 * degree + 1
-            number = (chunk - degree * degree) * TILES
+            number = (chunk - FIRST_CHUNK[degree]) * TILES
             segments = []
             t = 0
             while t < TILES:
@@ -81,23 +91,25 @@ def tile_linear_pa_kernel(tc, x, weights, path_weights, grad_out, out):
             g_rows = grad_out.rearrange("n m k -> n (m k)")
             raw = raw_pool.tile([P, TILES * K], BF16, name="raw%d" % chunk, offset=chunk * RAW_BYTES)
             for t, node_tile, m, rows in segments_of(chunk):
-                nc.sync.dma_start(
-                    out=raw[:, t * K : (t + rows) * K],
-                    in_=g_rows[node_tile * P : (node_tile + 1) * P, m * K : (m + rows) * K],
-                )
+                step = 1 if chunk < FINE_LOADS else rows
+                for r in range(0, rows, step):
+                    nc.sync.dma_start(
+                        out=raw[:, (t + r) * K : (t + r + step) * K],
+                        in_=g_rows[node_tile * P : (node_tile + 1) * P, (m + r) * K : (m + r + step) * K],
+                    )
             return raw
 
         def is_first_of_degree(chunk):
-            return chunk == DEGREE_OF_CHUNK[chunk] * DEGREE_OF_CHUNK[chunk]
+            return chunk == FIRST_CHUNK[DEGREE_OF_CHUNK[chunk]]
 
         raw_of_chunk = []
-        raw_of_degree = [load_weights(0)]
+        raw_of_degree = {DEGREE_ORDER[0]: load_weights(DEGREE_ORDER[0])}
 
         def load_next_chunk():
             chunk = len(raw_of_chunk)
             raw_of_chunk.append(load_grad(chunk))
             if chunk > 0 and is_first_of_degree(chunk):
-                raw_of_degree.append(load_weights(DEGREE_OF_CHUNK[chunk]))
+                raw_of_degree[DEGREE_OF_CHUNK[chunk]] = load_weights(DEGREE_OF_CHUNK[chunk])
 
         for chunk in range(LOADS_AHEAD):
             load_next_chunk()
@@ -140,7 +152,7 @@ def tile_linear_pa_kernel(tc, x, weights, path_weights, grad_out, out):
             degree = DEGREE_OF_CHUNK[chunk]
             products = []
             for half in range(CIN_HALVES):
-                acc = acc_psum.tile([P, TILES * P], F32)
+                acc = acc_psum.tile([P, TILES * P], F32, tag="acc")
                 for c in range(PASSES):
                     w_first = (degree * PASSES + c) * CIN + half * P
                     w_columns = slice(w_first, w_first + P)
@@ -182,7 +194,7 @@ def tile_linear_pa_kernel(tc, x, weights, path_weights, grad_out, out):
                     in_=result[:, t * CIN : (t + rows) * CIN],
                 )
 
-        quantise_weights(0)
+        quantise_weights(DEGREE_ORDER[0])
         ahead = quantise_grad(transpose_tiles(raw_of_chunk[0], TILES))
         products = []
         for chunk in range(G_CHUNKS):

@@ -117,7 +117,11 @@ def tile_linear_pa_kernel(tc, x, weights, path_weights, grad_out, out):
         w_codes = const.tile([P, DEGREES * PASSES * CIN], U32, align_bytes=64)
         w_scales = const.tile([P, DEGREES * PASSES * CIN], U8, align_bytes=64)
 
-        def transpose_tiles(raw, tiles):
+        def keep_busy():
+            unread = acc_psum.tile([P, TILES * P], F32, tag="acc")
+            nc.tensor.matmul(out=unread[:], lhsT=zeros[:, :P], rhs=zeros[:], start=True, stop=True)
+
+        def transpose_tiles(raw, tiles, starved):
             grouped = grouped_pool.tile([P, tiles * K], BF16, align_bytes=64)
             grouped_words = grouped[:].bitcast(F32).rearrange(
                 "q (c t r u) -> q c t r u", c=PASSES, t=tiles, u=2
@@ -128,6 +132,8 @@ def tile_linear_pa_kernel(tc, x, weights, path_weights, grad_out, out):
                 for h in range(QUARTERS):
                     first = (t * QUARTERS + h) * P
                     nc.tensor.transpose(bank[:, h, :], raw_words[:, first : first + P], identity[:])
+                if starved:
+                    keep_busy()
                 paired = bank[:].rearrange("q (c u) r -> q c r u", u=2)
                 if t < SCALAR_TILES:
                     nc.scalar.copy(out=grouped_words[:, :, t, :, :], in_=paired)
@@ -137,7 +143,7 @@ def tile_linear_pa_kernel(tc, x, weights, path_weights, grad_out, out):
 
         def quantise_weights(degree):
             columns = slice(degree * PASSES * CIN, (degree + 1) * PASSES * CIN)
-            grouped = transpose_tiles(raw_of_degree[degree], CIN_HALVES)
+            grouped = transpose_tiles(raw_of_degree[degree], CIN_HALVES, degree == DEGREE_ORDER[0])
             nc.vector.quantize_mx(
                 out=w_codes[:, columns].bitcast(E4M3_X4), scales=w_scales[:, columns], in_=grouped[:]
             )
@@ -195,7 +201,7 @@ def tile_linear_pa_kernel(tc, x, weights, path_weights, grad_out, out):
                 )
 
         quantise_weights(DEGREE_ORDER[0])
-        ahead = quantise_grad(transpose_tiles(raw_of_chunk[0], TILES))
+        ahead = quantise_grad(transpose_tiles(raw_of_chunk[0], TILES, True))
         products = []
         for chunk in range(G_CHUNKS):
             if len(raw_of_chunk) < G_CHUNKS:
@@ -204,7 +210,7 @@ def tile_linear_pa_kernel(tc, x, weights, path_weights, grad_out, out):
             if chunk > 0 and is_first_of_degree(chunk):
                 quantise_weights(DEGREE_OF_CHUNK[chunk])
             if chunk + 1 < G_CHUNKS:
-                grouped_ahead = transpose_tiles(raw_of_chunk[chunk + 1], TILES)
+                grouped_ahead = transpose_tiles(raw_of_chunk[chunk + 1], TILES, chunk + 1 < FINE_LOADS)
             if chunk > 0:
                 store_chunk(chunk - 1, products)
             if chunk + 1 < G_CHUNKS:

from contextlib import ExitStack

import concourse.mybir as mybir
from concourse.masks import make_identity

F32 = mybir.dt.float32
BF16 = mybir.dt.bfloat16
U32 = mybir.dt.uint32
U8 = mybir.dt.uint8
E4M3_X4 = mybir.dt.float8_e4m3fn_x4
E5M2_X4 = mybir.dt.float8_e5m2_x4

P = 128
NODES, DEGREES, CIN, K = 512, 4, 256, 1024
ROWS = DEGREES * DEGREES
G_CHUNKS = ROWS
DEGREE_ORDER = [3, 2, 1, 0]
DEGREE_OF_CHUNK = [l for l in DEGREE_ORDER for chunk in range(2 * l + 1)]
FIRST_CHUNK = [DEGREE_OF_CHUNK.index(l) for l in range(DEGREES)]

K_PASS = 4 * P
PASSES = K // K_PASS
QUARTERS = K // 2 // P
TILES = NODES // P
CIN_HALVES = CIN // P
PAIR = 2
SCALAR_TILES = 3
WARM_UP_MATMULS = 5
FINE_LOADS = 2
RAW_BYTES = 2 * TILES * K
LOADS_AHEAD = G_CHUNKS

FLOPS = 2 * NODES * ROWS * CIN * K
BYTES = 2 * NODES * ROWS * K + 2 * DEGREES * CIN * K + 2 * DEGREES + 4 * NODES * ROWS * CIN


def tile_linear_pa_kernel(tc, x, weights, path_weights, grad_out, out):
    nc = tc.nc
    assert tuple(grad_out.shape) == (NODES, ROWS, K)
    assert tuple(weights.shape) == (DEGREES, CIN, K)
    assert tuple(out.shape) == (NODES, ROWS, CIN)

    with ExitStack() as ctx:
        ctx.enter_context(tc.manual_schedule())
        const = ctx.enter_context(tc.tile_pool(name="const", bufs=1))
        raw_pool = ctx.enter_context(tc.tile_pool(name="raw", bufs=1))
        w_raw_pool = ctx.enter_context(tc.tile_pool(name="w_raw", bufs=DEGREES))
        grouped_pool = ctx.enter_context(tc.tile_pool(name="grouped", bufs=2))
        codes_pool = ctx.enter_context(tc.tile_pool(name="codes", bufs=2))
        product_pool = ctx.enter_context(tc.tile_pool(name="product", bufs=2 * CIN_HALVES))
        words_psum = ctx.enter_context(tc.psum_pool(name="words_psum", bufs=TILES))
        acc_psum = ctx.enter_context(tc.psum_pool(name="acc_psum", bufs=CIN_HALVES))
        back_psum = ctx.enter_context(tc.psum_pool(name="back_psum", bufs=TILES // PAIR))

        zeros = const.tile([P, TILES * P], BF16)
        nc.vector.memset(zeros[:], 0.0)
        for i in range(WARM_UP_MATMULS):
            unread = acc_psum.tile([P, TILES * P], F32, tag="acc")
            nc.tensor.matmul(out=unread[:], lhsT=zeros[:, :P], rhs=zeros[:], start=True, stop=True)

        identity = const.tile([P, P], F32)
        make_identity(nc, identity[:])
        factor_bf16 = const.tile([P, DEGREES], BF16)
        nc.scalar.dma_start(out=factor_bf16[:], in_=path_weights.partition_broadcast(P))
        factor = const.tile([P, DEGREES], F32)
        nc.vector.tensor_copy(out=factor[:], in_=factor_bf16[:])

        def load_weights(degree):
            w_raw = w_raw_pool.tile([P, CIN_HALVES * K], BF16)
            for half in range(CIN_HALVES):
                nc.sync.dma_start(
                    out=w_raw[:, half * K : (half + 1) * K],
                    in_=weights[degree, half * P : (half + 1) * P, :],
                )
            return w_raw

        def segments_of(chunk):
            degree = DEGREE_OF_CHUNK[chunk]
            width = 2 * degree + 1
            number = (chunk - FIRST_CHUNK[degree]) * TILES
            segments = []
            t = 0
            while t < TILES:
                node_tile, row = divmod(number + t, width)
                rows = min(TILES - t, width - row)
                segments.append((t, node_tile, degree * degree + row, rows))
                t += rows
            return segments

        def load_grad(chunk):
            g_rows = grad_out.rearrange("n m k -> n (m k)")
            raw = raw_pool.tile([P, TILES * K], BF16, name="raw%d" % chunk, offset=chunk * RAW_BYTES)
            for t, node_tile, m, rows in segments_of(chunk):
                step = 1 if chunk < FINE_LOADS else rows
                for r in range(0, rows, step):
                    nc.sync.dma_start(
                        out=raw[:, (t + r) * K : (t + r + step) * K],
                        in_=g_rows[node_tile * P : (node_tile + 1) * P, (m + r) * K : (m + r + step) * K],
                    )
            return raw

        def is_first_of_degree(chunk):
            return chunk == FIRST_CHUNK[DEGREE_OF_CHUNK[chunk]]

        raw_of_chunk = []
        raw_of_degree = {DEGREE_ORDER[0]: load_weights(DEGREE_ORDER[0])}

        def load_next_chunk():
            chunk = len(raw_of_chunk)
            raw_of_chunk.append(load_grad(chunk))
            if chunk > 0 and is_first_of_degree(chunk):
                raw_of_degree[DEGREE_OF_CHUNK[chunk]] = load_weights(DEGREE_OF_CHUNK[chunk])

        for chunk in range(LOADS_AHEAD):
            load_next_chunk()

        w_codes = const.tile([P, DEGREES * PASSES * CIN], U32, align_bytes=64)
        w_scales = const.tile([P, DEGREES * PASSES * CIN], U8, align_bytes=64)

        def keep_busy():
            unread = acc_psum.tile([P, TILES * P], F32, tag="acc")
            nc.tensor.matmul(out=unread[:], lhsT=zeros[:, :P], rhs=zeros[:], start=True, stop=True)

        def transpose_tiles(raw, tiles, starved):
            grouped = grouped_pool.tile([P, tiles * K], BF16, align_bytes=64)
            grouped_words = grouped[:].bitcast(F32).rearrange(
                "q (c t r u) -> q c t r u", c=PASSES, t=tiles, u=2
            )
            raw_words = raw[:].bitcast(F32)
            for t in range(tiles):
                bank = words_psum.tile([P, QUARTERS, P], F32)
                for h in range(QUARTERS):
                    first = (t * QUARTERS + h) * P
                    nc.tensor.transpose(bank[:, h, :], raw_words[:, first : first + P], identity[:])
                if starved:
                    keep_busy()
                paired = bank[:].rearrange("q (c u) r -> q c r u", u=2)
                if t < SCALAR_TILES:
                    nc.scalar.copy(out=grouped_words[:, :, t, :, :], in_=paired)
                else:
                    nc.vector.tensor_copy(out=grouped_words[:, :, t, :, :], in_=paired)
            return grouped

        def quantise_weights(degree):
            columns = slice(degree * PASSES * CIN, (degree + 1) * PASSES * CIN)
            grouped = transpose_tiles(raw_of_degree[degree], CIN_HALVES, degree == DEGREE_ORDER[0])
            nc.vector.quantize_mx(
                out=w_codes[:, columns].bitcast(E4M3_X4), scales=w_scales[:, columns], in_=grouped[:]
            )

        def quantise_grad(grouped):
            g_codes = codes_pool.tile([P, PASSES * TILES * P], U32, align_bytes=64)
            g_scales = codes_pool.tile([P, PASSES * TILES * P], U8, align_bytes=64)
            nc.vector.quantize_mx(out=g_codes[:].bitcast(E5M2_X4), scales=g_scales[:], in_=grouped[:])
            return g_codes, g_scales

        def multiply(chunk, g_codes, g_scales):
            degree = DEGREE_OF_CHUNK[chunk]
            products = []
            for half in range(CIN_HALVES):
                acc = acc_psum.tile([P, TILES * P], F32, tag="acc")
                for c in range(PASSES):
                    w_first = (degree * PASSES + c) * CIN + half * P
                    w_columns = slice(w_first, w_first + P)
                    g_columns = slice(c * TILES * P, (c + 1) * TILES * P)
                    nc.tensor.matmul_mx(
                        out=acc[:],
                        lhsT=w_codes[:, w_columns].bitcast(E4M3_X4),
                        lhsT_scale=w_scales[:, w_columns],
                        rhs=g_codes[:, g_columns].bitcast(E5M2_X4),
                        rhs_scale=g_scales[:, g_columns],
                        start=(c == 0),
                        stop=(c == PASSES - 1),
                    )
                product = product_pool.tile([P, TILES * P], F32)
                nc.scalar.copy(out=product[:], in_=acc[:])
                products.append(product)
            return products

        def store_chunk(chunk, products):
            degree = DEGREE_OF_CHUNK[chunk]
            result = raw_pool.tile([P, TILES * CIN], F32, name="result%d" % chunk, offset=chunk * RAW_BYTES)
            for pair in range(TILES // PAIR):
                back = back_psum.tile([P, PAIR, CIN_HALVES, P], F32)
                for i in range(PAIR):
                    t = pair * PAIR + i
                    for half in range(CIN_HALVES):
                        nc.tensor.transpose(
                            back[:, i, half, :], products[half][:, t * P : (t + 1) * P], identity[:]
                        )
                nc.vector.tensor_scalar_mul(
                    out=result[:, pair * PAIR * CIN : (pair + 1) * PAIR * CIN],
                    in0=back[:].rearrange("p i h c -> p (i h c)"),
                    scalar1=factor[:, degree : degree + 1],
                )
            out_rows = out.rearrange("n m c -> n (m c)")
            for t, node_tile, m, rows in segments_of(chunk):
                nc.sync.dma_start(
                    out=out_rows[node_tile * P : (node_tile + 1) * P, m * CIN : (m + rows) * CIN],
                    in_=result[:, t * CIN : (t + rows) * CIN],
                )

        quantise_weights(DEGREE_ORDER[0])
        ahead = quantise_grad(transpose_tiles(raw_of_chunk[0], TILES, True))
        products = []
        for chunk in range(G_CHUNKS):
            if len(raw_of_chunk) < G_CHUNKS:
                load_next_chunk()
            current = ahead
            if chunk > 0 and is_first_of_degree(chunk):
                quantise_weights(DEGREE_OF_CHUNK[chunk])
            if chunk + 1 < G_CHUNKS:
                grouped_ahead = transpose_tiles(raw_of_chunk[chunk + 1], TILES, chunk + 1 < FINE_LOADS)
            if chunk > 0:
                store_chunk(chunk - 1, products)
            if chunk + 1 < G_CHUNKS:
                ahead = quantise_grad(grouped_ahead)
            products = multiply(chunk, current[0], current[1])
        store_chunk(G_CHUNKS - 1, products)
